import numpy as np
import ml_dtypes


def mxq(x, axis, fmt="e4m3"):
    dtype, down = {"e4m3": (ml_dtypes.float8_e4m3fn, 7), "e5m2": (ml_dtypes.float8_e5m2, 14)}[fmt]
    v = np.moveaxis(np.asarray(x, np.float32).astype(ml_dtypes.bfloat16).astype(np.float64), axis, -1)
    blocks = v.reshape(v.shape[:-1] + (-1, 32))
    amax = np.abs(blocks).max(-1, keepdims=True)
    byte = np.maximum(np.where(amax > 0, np.frexp(amax)[1] - 1 + 127, 0) - down, 1)
    scale = np.exp2(byte - 127.0)
    codes = (blocks / scale).astype(np.float32).astype(dtype).astype(np.float64)
    return np.moveaxis((codes * scale).reshape(v.shape), -1, axis)


WIDE = False


def mx_kscale(k):
    if not WIDE:
        return np.ones(k)
    levels = np.array([10, -10, 5, -5, 0])
    if k % 512:
        return np.exp2(np.random.permutation(np.resize(levels, k // 32))).repeat(32)
    a = np.empty((k // 512, 16))
    for p in range(k // 512):
        a[p, :8] = np.random.permutation(np.resize(levels, 8))
        for g in range(8):
            far = levels[np.abs(levels - a[p, g]) >= 10]
            a[p, g + 8] = far[np.random.randint(len(far))]
    return np.exp2(a.ravel()).repeat(32)


BF16 = ml_dtypes.bfloat16


def bf(x):
    return np.asarray(x, np.float32).astype(BF16)


def f64(x):
    return np.asarray(x).astype(np.float64)


B, T, C, HQ, HKV, HD = 4, 256, 2048, 16, 4, 128
E = HQ * HD


def sigmoid(v):
    return 1.0 / (1.0 + np.exp(-v))


def setup_inputs():
    t = mx_kscale(E)
    return {"attn": bf(np.random.standard_normal((B, T, HQ, HD)) * 0.5 * t.reshape(HQ, HD)),
            "Wg": bf(np.random.standard_normal((HD, HD)) * 2.0 / np.sqrt(HD) / t.max()),
            "bg": bf(np.random.standard_normal(HD) * 0.3),
            "Wo": bf(np.random.standard_normal((C, E)) * 2.0 / np.sqrt(E) / t),
            "bo": bf(np.random.standard_normal(C) * 0.1)}


def reference(attn, Wg, bg, Wo, bo):
    a = f64(attn)
    gate = sigmoid(a @ f64(Wg).T + f64(bg))
    h = (a * gate).reshape(B * T, E)
    return ((mxq(h, 1, "e4m3") @ mxq(f64(Wo), 1, "e4m3").T) + f64(bo)).reshape(B, T, C)

@@ -1,0 +1,273 @@
+from contextlib import ExitStack
+
+import concourse.mybir as mybir
+from concourse.masks import make_identity
+
+BF16 = mybir.dt.bfloat16
+F32 = mybir.dt.float32
+U32 = mybir.dt.uint32
+U8 = mybir.dt.uint8
+FP8X4 = mybir.dt.float8_e4m3fn_x4
+SIGMOID = mybir.ActivationFunctionType.Sigmoid
+MULT = mybir.AluOpType.mult
+ADD = mybir.AluOpType.add
+
+P = 128
+TOKENS = 4 * 256
+HEADS = 16
+E = HEADS * P
+C = 2048
+PACK = 4
+K_PASS = P * PACK
+PASSES = E // K_PASS
+TILES = TOKENS // P
+PAIR = 2 * P
+PAIRS = TOKENS // PAIR
+CHUNK = 512
+CHUNKS = C // CHUNK
+HALF = 256
+HALVES = C // HALF
+QUAD = 32
+
+FLOPS = 2 * TOKENS * E * C + 2 * TOKENS * HEADS * P * P
+
+
+def tile_gqaselfattention_pb_kernel(tc, attn, Wg, bg, Wo, bo, out):
+    nc = tc.nc
+    attn_rows = attn.rearrange("b t h d -> (b t) (h d)")
+    out_rows = out.rearrange("b t c -> (b t) c")
+
+    with ExitStack() as ctx:
+        keep = ctx.enter_context(tc.tile_pool(name="keep", bufs=1))
+        tok_pool = ctx.enter_context(tc.tile_pool(name="tok", bufs=4))
+        wo_pool = ctx.enter_context(tc.tile_pool(name="wo", bufs=10))
+        feat_pool = ctx.enter_context(tc.tile_pool(name="feat", bufs=3))
+        gate_pool = ctx.enter_context(tc.tile_pool(name="gate", bufs=4))
+        gated_pool = ctx.enter_context(tc.tile_pool(name="gated", bufs=2))
+        swapped_pool = ctx.enter_context(tc.tile_pool(name="swapped", bufs=2))
+        packed_pool = ctx.enter_context(tc.tile_pool(name="packed", bufs=3))
+        grouped_pool = ctx.enter_context(tc.tile_pool(name="grouped", bufs=3))
+        result_pool = ctx.enter_context(tc.tile_pool(name="result", bufs=8))
+        block_banks = ctx.enter_context(tc.psum_pool(name="blocks", bufs=4))
+        gate_banks = ctx.enter_context(tc.psum_pool(name="gates", bufs=2))
+        product_banks = ctx.enter_context(tc.psum_pool(name="products", bufs=2))
+
+        bo_all = keep.tile([P, C], BF16)
+        wg_in = keep.tile([P, P], BF16)
+        bg_in = keep.tile([P, P], BF16)
+        tokens_of = {}
+        wo_of = {}
+
+        def load_tokens(m):
+            tokens_of[m] = tok_pool.tile([P, E], BF16, name="tokens")
+            nc.sync.dma_start(out=tokens_of[m][:], in_=attn_rows[m * P : (m + 1) * P, :])
+
+        def load_wo(s):
+            wo_of[s] = wo_pool.tile([P, E], BF16, name="wo_rows")
+            nc.sync.dma_start(out=wo_of[s][:], in_=Wo[s * P : (s + 1) * P, :])
+
+        nc.vector.memset(bg_in[:], 0.0)
+        nc.scalar.dma_start(out=wg_in[:], in_=Wg)
+        nc.scalar.dma_start(out=bg_in[0:1, :], in_=bg.rearrange("(o f) -> o f", o=1))
+        load_tokens(0)
+        load_tokens(1)
+        for s in range(4):
+            load_wo(s)
+
+        warm = keep.tile([P, 1], F32)
+        nc.vector.memset(warm[:], 0.0)
+        nc.scalar.activation(out=warm[:], in_=warm[:], func=SIGMOID)
+
+        ident = keep.tile([P, P], BF16)
+        make_identity(nc, ident[:])
+        ident_words = keep.tile([P, P], F32)
+        make_identity(nc, ident_words[:])
+        wg_t = keep.tile([P, P], BF16)
+        bg_col = keep.tile([P, 1], F32)
+
+        def set_up_gate():
+            setup = block_banks.tile([P, 8 * P], BF16, name="setup", tag="blocks")
+            nc.tensor.transpose(out=setup[:, 0:P], in_=wg_in[:], identity=ident[:])
+            nc.tensor.transpose(out=setup[:, P : 2 * P], in_=bg_in[:], identity=ident[:])
+            nc.scalar.copy(out=wg_t[:], in_=setup[:, 0:P])
+            nc.scalar.copy(out=bg_col[:], in_=setup[:, P : P + 1])
+
+        h_codes = keep.tile([P, PAIRS, PASSES * PAIR], U32, align_bytes=64)
+        h_scales = keep.tile([P, PAIRS, PASSES * PAIR], U8, align_bytes=64)
+        wo_codes = keep.tile([P, PASSES, C], U32, align_bytes=64)
+        wo_scales = keep.tile([P, PASSES, C], U8, align_bytes=64)
+
+        feats_of = {}
+        gated_of = {}
+        swapped_of = {}
+        packed_of = {}
+        grouped_of = {}
+
+        def transpose_tokens(m):
+            feats_of[m] = feat_pool.tile([P, HEADS * P], BF16, name="feats")
+            for i in range(2):
+                bank = block_banks.tile([P, 8 * P], BF16, name="bank", tag="blocks")
+                for j in range(8):
+                    head = 8 * i + j
+                    nc.tensor.transpose(
+                        out=bank[:, j * P : (j + 1) * P],
+                        in_=tokens_of[m][:, head * P : (head + 1) * P],
+                        identity=ident[:],
+                    )
+                nc.scalar.copy(out=feats_of[m][:, i * 8 * P : (i + 1) * 8 * P], in_=bank[:])
+
+        def gate_tokens(m, j):
+            if m % 2 == 0 and j == 0:
+                gated_of[m // 2] = gated_pool.tile([P, HEADS, PAIR], BF16, name="gated")
+            a_t = feats_of[m][:, j * 4 * P : (j + 1) * 4 * P]
+            first = (m % 2) * P
+            h_t = gated_of[m // 2][:, 4 * j : 4 * j + 4, first : first + P]
+            z = gate_banks.tile([P, 4 * P], F32, name="z")
+            nc.tensor.matmul(out=z[:], lhsT=wg_t[:], rhs=a_t, start=True, stop=True)
+            gate = gate_pool.tile([P, 4 * P], F32, name="gate")
+            nc.scalar.activation(out=gate[:], in_=z[:], func=SIGMOID, bias=bg_col[:, 0:1])
+            nc.vector.tensor_tensor(
+                out=h_t,
+                in0=gate[:].rearrange("p (h c) -> p h c", h=4),
+                in1=a_t.rearrange("p (h c) -> p h c", h=4),
+                op=MULT,
+            )
+
+        def swap_pair(q):
+            swapped_of[q] = swapped_pool.tile([P, PACK, PASSES, PAIR], BF16, name="swapped")
+            heads = gated_of[q][:].rearrange("p (g i) c -> p i g c", i=4)
+            for t in range(PACK):
+                for i in range(4):
+                    nc.sync.dma_start(
+                        out=swapped_of[q][QUAD * i : QUAD * (i + 1), t, :, :],
+                        in_=heads[t : P : PACK, i, :, :],
+                    )
+
+        def pack_pair(q, half):
+            packed_of[q, half] = packed_pool.tile([P, 2 * PAIR * PACK], BF16, name="packed", align_bytes=64)
+            copy = nc.vector.tensor_copy if half == 0 else nc.scalar.copy
+            copy(
+                out=packed_of[q, half][:].rearrange("p (c t) -> p c t", t=PACK),
+                in_=swapped_of[q][:, :, 2 * half : 2 * half + 2, :].rearrange("p t g c -> p (g c) t"),
+            )
+
+        def quantise_pair(q, half):
+            cols = slice(half * 2 * PAIR, (half + 1) * 2 * PAIR)
+            nc.vector.quantize_mx(
+                out=h_codes[:, q, cols].bitcast(FP8X4), scales=h_scales[:, q, cols], in_=packed_of[q, half][:]
+            )
+
+        def transpose_wo(s, vector_helps):
+            w = s // 2
+            if s % 2 == 0:
+                grouped_of[w] = grouped_pool.tile([P, PASSES * HALF * PACK], BF16, name="grouped", align_bytes=64)
+            words_in = wo_of[s][:].bitcast(F32)
+            words_out = grouped_of[w][:].bitcast(F32).rearrange("p (g r u) -> p g r u", g=PASSES, u=2)
+            first = (s % 2) * P
+            for b in range(2):
+                bank = block_banks.tile([P, 4 * P], F32, name="bank", tag="blocks")
+                for j in range(2):
+                    g = 2 * b + j
+                    for u in range(2):
+                        place = 2 * j + u
+                        nc.tensor.transpose(
+                            out=bank[:, place * P : (place + 1) * P],
+                            in_=words_in[:, 256 * g + u : 256 * (g + 1) : 2],
+                            identity=ident_words[:],
+                        )
+                copy = nc.vector.tensor_copy if vector_helps and b == 1 else nc.scalar.copy
+                copy(
+                    out=words_out[:, 2 * b : 2 * b + 2, first : first + P, :],
+                    in_=bank[:].rearrange("p (g u r) -> p g r u", g=2, u=2),
+                )
+
+        def quantise_wo(w):
+            cols = slice(w * HALF, (w + 1) * HALF)
+            for g in range(PASSES):
+                nc.vector.quantize_mx(
+                    out=wo_codes[:, g, cols].bitcast(FP8X4),
+                    scales=wo_scales[:, g, cols],
+                    in_=grouped_of[w][:, g * HALF * PACK : (g + 1) * HALF * PACK],
+                )
+
+        def product(m, n):
+            cols = slice(n * CHUNK, (n + 1) * CHUNK)
+            acc = product_banks.tile([P, CHUNK], F32, name="acc")
+            for g in range(PASSES):
+                first = g * PAIR + (m % 2) * P
+                toks = slice(first, first + P)
+                nc.tensor.matmul_mx(
+                    out=acc[:],
+                    lhsT=h_codes[:, m // 2, toks].bitcast(FP8X4),
+                    lhsT_scale=h_scales[:, m // 2, toks],
+                    rhs=wo_codes[:, g, cols].bitcast(FP8X4),
+                    rhs_scale=wo_scales[:, g, cols],
+                    start=(g == 0),
+                    stop=(g == PASSES - 1),
+                )
+            result = result_pool.tile([P, CHUNK], F32, name="result")
+            nc.vector.tensor_tensor(out=result[:], in0=acc[:], in1=bo_all[:, cols], op=ADD)
+            nc.sync.dma_start(out=out_rows[m * P : (m + 1) * P, cols], in_=result[:])
+
+        waiting = []
+
+        def products(count):
+            for i in range(min(count, len(waiting))):
+                product(*waiting.pop(0))
+
+        def prepare_pair(q, count):
+            transpose_tokens(2 * q)
+            if q == 0:
+                set_up_gate()
+            for m in (2 * q, 2 * q + 1):
+                for j in range(4):
+                    gate_tokens(m, j)
+                    if j == 1 and m == 2 * q:
+                        transpose_tokens(2 * q + 1)
+                    if j % 2 == 1:
+                        products(count)
+            swap_pair(q)
+
+        def finish_pair(q):
+            pack_pair(q, 0)
+            pack_pair(q, 1)
+            quantise_pair(q, 0)
+            quantise_pair(q, 1)
+
+        def prepare_chunk(n, count, help_out):
+            for w in (2 * n, 2 * n + 1):
+                transpose_wo(2 * w, help_out)
+                transpose_wo(2 * w + 1, help_out)
+                products(count)
+                quantise_wo(w)
+
+        load_tokens(2)
+        load_tokens(3)
+        for s in range(4, 8):
+            load_wo(s)
+        nc.sync.dma_start(out=bo_all[:], in_=bo.partition_broadcast(P))
+        prepare_pair(0, 0)
+        prepare_chunk(0, 0, True)
+        for s in range(8, 12):
+            load_wo(s)
+        load_tokens(4)
+        load_tokens(5)
+        finish_pair(0)
+        waiting.extend([(0, 0), (1, 0)])
+        prepare_pair(1, 0)
+        prepare_chunk(1, 1, False)
+        for s in range(12, 16):
+            load_wo(s)
+        load_tokens(6)
+        load_tokens(7)
+        finish_pair(1)
+        waiting.extend([(0, 1), (1, 1), (2, 0), (3, 0), (2, 1), (3, 1)])
+        prepare_pair(2, 0)
+        prepare_chunk(2, 3, False)
+        finish_pair(2)
+        waiting.extend([(m, 2) for m in range(4)] + [(4, 0), (5, 0), (4, 1), (5, 1), (4, 2), (5, 2)])
+        prepare_pair(3, 1)
+        prepare_chunk(3, 2, False)
+        finish_pair(3)
+        waiting.extend([(m, 3) for m in range(6)] + [(m, n) for m in (6, 7) for n in range(CHUNKS)])
+        products(len(waiting))

@@ -45,13 +45,14 @@ def tile_gqaselfattention_pb_kernel(tc, attn, Wg, bg, Wo, bo, out):
         gate_pool = ctx.enter_context(tc.tile_pool(name="gate", bufs=4))
         gated_pool = ctx.enter_context(tc.tile_pool(name="gated", bufs=2))
         swapped_pool = ctx.enter_context(tc.tile_pool(name="swapped", bufs=2))
-        packed_pool = ctx.enter_context(tc.tile_pool(name="packed", bufs=3))
+        packed_pool = ctx.enter_context(tc.tile_pool(name="packed", bufs=2))
         grouped_pool = ctx.enter_context(tc.tile_pool(name="grouped", bufs=3))
         result_pool = ctx.enter_context(tc.tile_pool(name="result", bufs=8))
         block_banks = ctx.enter_context(tc.psum_pool(name="blocks", bufs=4))
         gate_banks = ctx.enter_context(tc.psum_pool(name="gates", bufs=2))
         product_banks = ctx.enter_context(tc.psum_pool(name="products", bufs=2))
 
+        ctx.enter_context(tc.manual_schedule())
         bo_all = keep.tile([P, C], BF16)
         wg_in = keep.tile([P, P], BF16)
         bg_in = keep.tile([P, P], BF16)
@@ -70,8 +71,9 @@ def tile_gqaselfattention_pb_kernel(tc, attn, Wg, bg, Wo, bo, out):
         nc.scalar.dma_start(out=wg_in[:], in_=Wg)
         nc.scalar.dma_start(out=bg_in[0:1, :], in_=bg.rearrange("(o f) -> o f", o=1))
         load_tokens(0)
+        load_wo(0)
         load_tokens(1)
-        for s in range(4):
+        for s in range(1, 10):
             load_wo(s)
 
         warm = keep.tile([P, 1], F32)
@@ -143,9 +145,9 @@ def tile_gqaselfattention_pb_kernel(tc, attn, Wg, bg, Wo, bo, out):
                         in_=heads[t : P : PACK, i, :, :],
                     )
 
-        def pack_pair(q, half):
+        def pack_pair(q, half, engine):
             packed_of[q, half] = packed_pool.tile([P, 2 * PAIR * PACK], BF16, name="packed", align_bytes=64)
-            copy = nc.vector.tensor_copy if half == 0 else nc.scalar.copy
+            copy = nc.vector.tensor_copy if engine == "v" else nc.scalar.copy
             copy(
                 out=packed_of[q, half][:].rearrange("p (c t) -> p c t", t=PACK),
                 in_=swapped_of[q][:, :, 2 * half : 2 * half + 2, :].rearrange("p t g c -> p (g c) t"),
@@ -157,7 +159,7 @@ def tile_gqaselfattention_pb_kernel(tc, attn, Wg, bg, Wo, bo, out):
                 out=h_codes[:, q, cols].bitcast(FP8X4), scales=h_scales[:, q, cols], in_=packed_of[q, half][:]
             )
 
-        def transpose_wo(s, vector_helps):
+        def transpose_wo(s, engines):
             w = s // 2
             if s % 2 == 0:
                 grouped_of[w] = grouped_pool.tile([P, PASSES * HALF * PACK], BF16, name="grouped", align_bytes=64)
@@ -175,7 +177,7 @@ def tile_gqaselfattention_pb_kernel(tc, attn, Wg, bg, Wo, bo, out):
                             in_=words_in[:, 256 * g + u : 256 * (g + 1) : 2],
                             identity=ident_words[:],
                         )
-                copy = nc.vector.tensor_copy if vector_helps and b == 1 else nc.scalar.copy
+                copy = nc.vector.tensor_copy if engines[b] == "v" else nc.scalar.copy
                 copy(
                     out=words_out[:, 2 * b : 2 * b + 2, first : first + P, :],
                     in_=bank[:].rearrange("p (g u r) -> p g r u", g=2, u=2),
@@ -205,69 +207,137 @@ def tile_gqaselfattention_pb_kernel(tc, attn, Wg, bg, Wo, bo, out):
                     start=(g == 0),
                     stop=(g == PASSES - 1),
                 )
+            return m, n, acc
+
+        def finish_product(m, n, acc):
+            cols = slice(n * CHUNK, (n + 1) * CHUNK)
             result = result_pool.tile([P, CHUNK], F32, name="result")
             nc.vector.tensor_tensor(out=result[:], in0=acc[:], in1=bo_all[:, cols], op=ADD)
             nc.sync.dma_start(out=out_rows[m * P : (m + 1) * P, cols], in_=result[:])
 
-        waiting = []
+        open_products = []
 
-        def products(count):
-            for i in range(min(count, len(waiting))):
-                product(*waiting.pop(0))
+        def close(left):
+            while len(open_products) > left:
+                finish_product(*open_products.pop(0))
 
-        def prepare_pair(q, count):
+        def run(m, n):
+            open_products.append(product(m, n))
+            close(0)
+
+        def gates(m, js):
+            for j in js:
+                gate_tokens(m, j)
+
+        def pair_with_products(q, first, second, third, fourth):
             transpose_tokens(2 * q)
-            if q == 0:
-                set_up_gate()
-            for m in (2 * q, 2 * q + 1):
-                for j in range(4):
-                    gate_tokens(m, j)
-                    if j == 1 and m == 2 * q:
-                        transpose_tokens(2 * q + 1)
-                    if j % 2 == 1:
-                        products(count)
+            transpose_tokens(2 * q + 1)
+            run(*first)
+            gates(2 * q, (0, 1))
+            run(*second)
+            gates(2 * q, (2, 3))
+            run(*third)
+            gates(2 * q + 1, (0, 1))
+            run(*fourth)
+            gates(2 * q + 1, (2, 3))
             swap_pair(q)
 
-        def finish_pair(q):
-            pack_pair(q, 0)
-            pack_pair(q, 1)
-            quantise_pair(q, 0)
-            quantise_pair(q, 1)
-
-        def prepare_chunk(n, count, help_out):
-            for w in (2 * n, 2 * n + 1):
-                transpose_wo(2 * w, help_out)
-                transpose_wo(2 * w + 1, help_out)
-                products(count)
-                quantise_wo(w)
-
+        transpose_tokens(0)
+        transpose_wo(0, "vv")
+        set_up_gate()
+        gates(0, (0, 1))
+        transpose_tokens(1)
+        gates(0, (2, 3))
+        transpose_wo(1, "vs")
+        gates(1, (0, 1))
+        transpose_wo(2, "vs")
+        gates(1, (2, 3))
+        swap_pair(0)
+        for s in range(10, 12):
+            load_wo(s)
         load_tokens(2)
         load_tokens(3)
-        for s in range(4, 8):
-            load_wo(s)
-        nc.sync.dma_start(out=bo_all[:], in_=bo.partition_broadcast(P))
-        prepare_pair(0, 0)
-        prepare_chunk(0, 0, True)
-        for s in range(8, 12):
-            load_wo(s)
         load_tokens(4)
         load_tokens(5)
-        finish_pair(0)
-        waiting.extend([(0, 0), (1, 0)])
-        prepare_pair(1, 0)
-        prepare_chunk(1, 1, False)
-        for s in range(12, 16):
-            load_wo(s)
+        nc.sync.dma_start(out=bo_all[:], in_=bo.partition_broadcast(P))
+        transpose_wo(3, "vs")
+        quantise_wo(0)
+        transpose_wo(4, "ss")
+        transpose_wo(5, "vs")
+        quantise_wo(1)
+        transpose_wo(6, "vs")
+        transpose_wo(7, "ss")
+        quantise_wo(2)
+        transpose_wo(8, "vs")
+        pack_pair(0, 0, "v")
+        transpose_wo(9, "ss")
+        pack_pair(0, 1, "v")
+        transpose_wo(10, "ss")
+        quantise_pair(0, 0)
+        quantise_pair(0, 1)
+        transpose_wo(11, "vs")
+        quantise_wo(3)
+        quantise_wo(4)
+        load_wo(12)
+        load_wo(13)
+        load_wo(14)
+        load_wo(15)
+        quantise_wo(5)
+
+        pair_with_products(1, (0, 0), (1, 0), (0, 1), (1, 1))
         load_tokens(6)
         load_tokens(7)
-        finish_pair(1)
-        waiting.extend([(0, 1), (1, 1), (2, 0), (3, 0), (2, 1), (3, 1)])
-        prepare_pair(2, 0)
-        prepare_chunk(2, 3, False)
-        finish_pair(2)
-        waiting.extend([(m, 2) for m in range(4)] + [(4, 0), (5, 0), (4, 1), (5, 1), (4, 2), (5, 2)])
-        prepare_pair(3, 1)
-        prepare_chunk(3, 2, False)
-        finish_pair(3)
-        waiting.extend([(m, 3) for m in range(6)] + [(m, n) for m in (6, 7) for n in range(CHUNKS)])
-        products(len(waiting))
+        transpose_wo(12, "ss")
+        transpose_wo(13, "ss")
+        run(0, 2)
+        run(1, 2)
+        quantise_wo(6)
+        transpose_wo(14, "sv")
+        transpose_wo(15, "sv")
+        quantise_wo(7)
+        pack_pair(1, 0, "v")
+        transpose_tokens(4)
+        transpose_tokens(5)
+        run(0, 3)
+        pack_pair(1, 1, "v")
+        quantise_pair(1, 0)
+        gates(4, (0, 1))
+        run(1, 3)
+        quantise_pair(1, 1)
+        gates(4, (2, 3))
+        run(2, 0)
+        gates(5, (0, 1))
+        run(3, 0)
+        gates(5, (2, 3))
+        swap_pair(2)
+        run(2, 1)
+        run(3, 1)
+        transpose_tokens(6)
+        transpose_tokens(7)
+        run(2, 2)
+        gates(6, (0, 1))
+        run(3, 2)
+        gates(6, (2, 3))
+        pack_pair(2, 0, "v")
+        run(2, 3)
+        gates(7, (0, 1))
+        pack_pair(2, 1, "s")
+        quantise_pair(2, 0)
+        run(3, 3)
+        gates(7, (2, 3))
+        swap_pair(3)
+        quantise_pair(2, 1)
+        for n in range(CHUNKS):
+            run(4, n)
+        for n in range(CHUNKS):
+            run(5, n)
+            if n == 0:
+                pack_pair(3, 0, "s")
+                pack_pair(3, 1, "v")
+            if n == 1:
+                quantise_pair(3, 0)
+                quantise_pair(3, 1)
+        for m in (6, 7):
+            for n in range(CHUNKS):
+                run(m, n)
+        close(0)

@@ -139,7 +139,7 @@ def tile_gqaselfattention_pb_kernel(tc, attn, Wg, bg, Wo, bo, out):
             swapped_of[q] = swapped_pool.tile([P, PACK, PASSES, PAIR], BF16, name="swapped")
             heads = gated_of[q][:].rearrange("p (g i) c -> p i g c", i=4)
             for t in range(PACK):
-                for i in range(4):
+                for i in (0, 2, 1, 3):
                     nc.sync.dma_start(
                         out=swapped_of[q][QUAD * i : QUAD * (i + 1), t, :, :],
                         in_=heads[t : P : PACK, i, :, :],

@@ -29,6 +29,9 @@ HALF = 256
 HALVES = C // HALF
 QUAD = 32
 
+COUNTS = [(0,0,0,0)]*5 + [(1,1,1,1)]*3
+DUMMY = [512]*5+[0]*3
+PACKS = [(),(),(),((0,0,"v"),(0,1,"v")),(),((1,0,"v"),(1,1,"v")),(),()]
 FLOPS = 2 * TOKENS * E * C + 2 * TOKENS * HEADS * P * P
 
 
@@ -39,7 +42,7 @@ def tile_gqaselfattention_pb_kernel(tc, attn, Wg, bg, Wo, bo, out):
 
     with ExitStack() as ctx:
         keep = ctx.enter_context(tc.tile_pool(name="keep", bufs=1))
-        tok_pool = ctx.enter_context(tc.tile_pool(name="tok", bufs=4))
+        tok_pool = ctx.enter_context(tc.tile_pool(name="tok", bufs=5))
         wo_pool = ctx.enter_context(tc.tile_pool(name="wo", bufs=10))
         feat_pool = ctx.enter_context(tc.tile_pool(name="feat", bufs=3))
         gate_pool = ctx.enter_context(tc.tile_pool(name="gate", bufs=4))
@@ -47,15 +50,15 @@ def tile_gqaselfattention_pb_kernel(tc, attn, Wg, bg, Wo, bo, out):
         swapped_pool = ctx.enter_context(tc.tile_pool(name="swapped", bufs=2))
         packed_pool = ctx.enter_context(tc.tile_pool(name="packed", bufs=2))
         grouped_pool = ctx.enter_context(tc.tile_pool(name="grouped", bufs=3))
-        result_pool = ctx.enter_context(tc.tile_pool(name="result", bufs=8))
+        result_pool = ctx.enter_context(tc.tile_pool(name="result", bufs=7))
         block_banks = ctx.enter_context(tc.psum_pool(name="blocks", bufs=4))
         gate_banks = ctx.enter_context(tc.psum_pool(name="gates", bufs=2))
         product_banks = ctx.enter_context(tc.psum_pool(name="products", bufs=2))
 
-        ctx.enter_context(tc.manual_schedule())
+        ctx.enter_context(tc.manual_schedule(engines={mybir.EngineType.PE, mybir.EngineType.SP}))
         bo_all = keep.tile([P, C], BF16)
         wg_in = keep.tile([P, P], BF16)
-        bg_in = keep.tile([P, P], BF16)
+        bg_col = keep.tile([P, 1], BF16)
         tokens_of = {}
         wo_of = {}
 
@@ -67,32 +70,23 @@ def tile_gqaselfattention_pb_kernel(tc, attn, Wg, bg, Wo, bo, out):
             wo_of[s] = wo_pool.tile([P, E], BF16, name="wo_rows")
             nc.sync.dma_start(out=wo_of[s][:], in_=Wo[s * P : (s + 1) * P, :])
 
-        nc.vector.memset(bg_in[:], 0.0)
+        ident = keep.tile([P, P], BF16)
+        make_identity(nc, ident[:])
+        ident_words = keep.tile([P, P], F32)
+        make_identity(nc, ident_words[:])
         nc.scalar.dma_start(out=wg_in[:], in_=Wg)
-        nc.scalar.dma_start(out=bg_in[0:1, :], in_=bg.rearrange("(o f) -> o f", o=1))
-        load_tokens(0)
-        load_wo(0)
-        load_tokens(1)
-        for s in range(1, 10):
-            load_wo(s)
+        nc.scalar.dma_start(out=bg_col[:], in_=bg.rearrange("(f o) -> f o", o=1))
 
         warm = keep.tile([P, 1], F32)
         nc.vector.memset(warm[:], 0.0)
         nc.scalar.activation(out=warm[:], in_=warm[:], func=SIGMOID)
 
-        ident = keep.tile([P, P], BF16)
-        make_identity(nc, ident[:])
-        ident_words = keep.tile([P, P], F32)
-        make_identity(nc, ident_words[:])
         wg_t = keep.tile([P, P], BF16)
-        bg_col = keep.tile([P, 1], F32)
 
         def set_up_gate():
             setup = block_banks.tile([P, 8 * P], BF16, name="setup", tag="blocks")
             nc.tensor.transpose(out=setup[:, 0:P], in_=wg_in[:], identity=ident[:])
-            nc.tensor.transpose(out=setup[:, P : 2 * P], in_=bg_in[:], identity=ident[:])
-            nc.scalar.copy(out=wg_t[:], in_=setup[:, 0:P])
-            nc.scalar.copy(out=bg_col[:], in_=setup[:, P : P + 1])
+            nc.vector.tensor_copy(out=wg_t[:], in_=setup[:, 0:P])
 
         h_codes = keep.tile([P, PAIRS, PASSES * PAIR], U32, align_bytes=64)
         h_scales = keep.tile([P, PAIRS, PASSES * PAIR], U8, align_bytes=64)
@@ -105,9 +99,10 @@ def tile_gqaselfattention_pb_kernel(tc, attn, Wg, bg, Wo, bo, out):
         packed_of = {}
         grouped_of = {}
 
-        def transpose_tokens(m):
-            feats_of[m] = feat_pool.tile([P, HEADS * P], BF16, name="feats")
-            for i in range(2):
+        def transpose_tokens(m, i, engine):
+            if i == 0:
+                feats_of[m] = feat_pool.tile([P, HEADS * P], BF16, name="feats")
+            if True:
                 bank = block_banks.tile([P, 8 * P], BF16, name="bank", tag="blocks")
                 for j in range(8):
                     head = 8 * i + j
@@ -116,9 +111,10 @@ def tile_gqaselfattention_pb_kernel(tc, attn, Wg, bg, Wo, bo, out):
                         in_=tokens_of[m][:, head * P : (head + 1) * P],
                         identity=ident[:],
                     )
-                nc.scalar.copy(out=feats_of[m][:, i * 8 * P : (i + 1) * 8 * P], in_=bank[:])
+                copy = nc.vector.tensor_copy if engine == "v" else nc.scalar.copy
+                copy(out=feats_of[m][:, i * 8 * P : (i + 1) * 8 * P], in_=bank[:])
 
-        def gate_tokens(m, j):
+        def gate_tokens(m, j, engine):
             if m % 2 == 0 and j == 0:
                 gated_of[m // 2] = gated_pool.tile([P, HEADS, PAIR], BF16, name="gated")
             a_t = feats_of[m][:, j * 4 * P : (j + 1) * 4 * P]
@@ -128,14 +124,14 @@ def tile_gqaselfattention_pb_kernel(tc, attn, Wg, bg, Wo, bo, out):
             nc.tensor.matmul(out=z[:], lhsT=wg_t[:], rhs=a_t, start=True, stop=True)
             gate = gate_pool.tile([P, 4 * P], F32, name="gate")
             nc.scalar.activation(out=gate[:], in_=z[:], func=SIGMOID, bias=bg_col[:, 0:1])
-            nc.vector.tensor_tensor(
+            (nc.gpsimd if engine == "g" else nc.vector).tensor_tensor(
                 out=h_t,
                 in0=gate[:].rearrange("p (h c) -> p h c", h=4),
                 in1=a_t.rearrange("p (h c) -> p h c", h=4),
                 op=MULT,
             )
 
-        def swap_pair(q):
+        def swap_pair(q, between=()):
             swapped_of[q] = swapped_pool.tile([P, PACK, PASSES, PAIR], BF16, name="swapped")
             heads = gated_of[q][:].rearrange("p (g i) c -> p i g c", i=4)
             for t in range(PACK):
@@ -144,6 +140,8 @@ def tile_gqaselfattention_pb_kernel(tc, attn, Wg, bg, Wo, bo, out):
                         out=swapped_of[q][QUAD * i : QUAD * (i + 1), t, :, :],
                         in_=heads[t : P : PACK, i, :, :],
                     )
+                if t < len(between):
+                    between[t]()
 
         def pack_pair(q, half, engine):
             packed_of[q, half] = packed_pool.tile([P, 2 * PAIR * PACK], BF16, name="packed", align_bytes=64)
@@ -159,14 +157,14 @@ def tile_gqaselfattention_pb_kernel(tc, attn, Wg, bg, Wo, bo, out):
                 out=h_codes[:, q, cols].bitcast(FP8X4), scales=h_scales[:, q, cols], in_=packed_of[q, half][:]
             )
 
-        def transpose_wo(s, engines):
+        def transpose_wo(s, b, engine):
             w = s // 2
-            if s % 2 == 0:
+            if s % 2 == 0 and b == 0:
                 grouped_of[w] = grouped_pool.tile([P, PASSES * HALF * PACK], BF16, name="grouped", align_bytes=64)
             words_in = wo_of[s][:].bitcast(F32)
             words_out = grouped_of[w][:].bitcast(F32).rearrange("p (g r u) -> p g r u", g=PASSES, u=2)
             first = (s % 2) * P
-            for b in range(2):
+            if True:
                 bank = block_banks.tile([P, 4 * P], F32, name="bank", tag="blocks")
                 for j in range(2):
                     g = 2 * b + j
@@ -177,7 +175,7 @@ def tile_gqaselfattention_pb_kernel(tc, attn, Wg, bg, Wo, bo, out):
                             in_=words_in[:, 256 * g + u : 256 * (g + 1) : 2],
                             identity=ident_words[:],
                         )
-                copy = nc.vector.tensor_copy if engines[b] == "v" else nc.scalar.copy
+                copy = nc.vector.tensor_copy if engine == "v" else nc.scalar.copy
                 copy(
                     out=words_out[:, 2 * b : 2 * b + 2, first : first + P, :],
                     in_=bank[:].rearrange("p (g u r) -> p g r u", g=2, u=2),
@@ -229,115 +227,89 @@ def tile_gqaselfattention_pb_kernel(tc, attn, Wg, bg, Wo, bo, out):
             for j in js:
                 gate_tokens(m, j)
 
-        def pair_with_products(q, first, second, third, fourth):
-            transpose_tokens(2 * q)
-            transpose_tokens(2 * q + 1)
-            run(*first)
-            gates(2 * q, (0, 1))
-            run(*second)
-            gates(2 * q, (2, 3))
-            run(*third)
-            gates(2 * q + 1, (0, 1))
-            run(*fourth)
-            gates(2 * q + 1, (2, 3))
-            swap_pair(q)
+        idle = keep.tile([P, CHUNK], BF16)
+        nc.vector.memset(idle[:], 0.0)
 
-        transpose_tokens(0)
-        transpose_wo(0, "vv")
+        def keep_clock(count, width=CHUNK):
+            for i in range(count):
+                nothing = gate_banks.tile([P, CHUNK], F32, name="z")
+                nc.tensor.matmul(out=nothing[:, 0:width], lhsT=idle[:, 0:P], rhs=idle[:, 0:width], start=True, stop=True)
+
+
+        waiting = []
+
+        def products(count):
+            for i in range(min(count, len(waiting))):
+                run(*waiting.pop(0))
+
+        def next_tokens(m, i, engine):
+            if m < TILES:
+                transpose_tokens(m, i, engine)
+
+        def load_round(r):
+            if r < TILES:
+                load_wo(2 * r)
+                if r + 1 < TILES:
+                    load_tokens(r + 1)
+                load_wo(2 * r + 1)
+
+        load_tokens(0)
+        for r in range(4):
+            load_round(r)
+            if r == 2:
+                nc.sync.dma_start(out=bo_all[:], in_=bo.partition_broadcast(P))
+        keep_clock(5)
         set_up_gate()
-        gates(0, (0, 1))
-        transpose_tokens(1)
-        gates(0, (2, 3))
-        transpose_wo(1, "vs")
-        gates(1, (0, 1))
-        transpose_wo(2, "vs")
-        gates(1, (2, 3))
-        swap_pair(0)
-        for s in range(10, 12):
-            load_wo(s)
-        load_tokens(2)
-        load_tokens(3)
-        load_tokens(4)
-        load_tokens(5)
-        nc.sync.dma_start(out=bo_all[:], in_=bo.partition_broadcast(P))
-        transpose_wo(3, "vs")
-        quantise_wo(0)
-        transpose_wo(4, "ss")
-        transpose_wo(5, "vs")
-        quantise_wo(1)
-        transpose_wo(6, "vs")
-        transpose_wo(7, "ss")
-        quantise_wo(2)
-        transpose_wo(8, "vs")
-        pack_pair(0, 0, "v")
-        transpose_wo(9, "ss")
-        pack_pair(0, 1, "v")
-        transpose_wo(10, "ss")
-        quantise_pair(0, 0)
-        quantise_pair(0, 1)
-        transpose_wo(11, "vs")
-        quantise_wo(3)
-        quantise_wo(4)
-        load_wo(12)
-        load_wo(13)
-        load_wo(14)
-        load_wo(15)
-        quantise_wo(5)
-
-        pair_with_products(1, (0, 0), (1, 0), (0, 1), (1, 1))
-        load_tokens(6)
-        load_tokens(7)
-        transpose_wo(12, "ss")
-        transpose_wo(13, "ss")
-        run(0, 2)
-        run(1, 2)
-        quantise_wo(6)
-        transpose_wo(14, "sv")
-        transpose_wo(15, "sv")
-        quantise_wo(7)
-        pack_pair(1, 0, "v")
-        transpose_tokens(4)
-        transpose_tokens(5)
-        run(0, 3)
-        pack_pair(1, 1, "v")
-        quantise_pair(1, 0)
-        gates(4, (0, 1))
-        run(1, 3)
-        quantise_pair(1, 1)
-        gates(4, (2, 3))
-        run(2, 0)
-        gates(5, (0, 1))
-        run(3, 0)
-        gates(5, (2, 3))
-        swap_pair(2)
-        run(2, 1)
-        run(3, 1)
-        transpose_tokens(6)
-        transpose_tokens(7)
-        run(2, 2)
-        gates(6, (0, 1))
-        run(3, 2)
-        gates(6, (2, 3))
+        transpose_tokens(0, 0, "s")
+        keep_clock(1)
+        transpose_tokens(0, 1, "v")
+        keep_clock(1)
+        for r in range(TILES):
+            a, b, c, d = COUNTS[r]
+            transpose_wo(2 * r, 0, "s")
+            products(a)
+            gate_tokens(r, 0, "g")
+            transpose_wo(2 * r, 1, "v")
+            next_tokens(r + 1, 0, "s")
+            products(b)
+            if r > 0:
+                quantise_wo(r - 1)
+            gate_tokens(r, 1, "v")
+            keep_clock(1 if DUMMY[r] else 0, DUMMY[r])
+            transpose_wo(2 * r + 1, 0, "s")
+            products(c)
+            gate_tokens(r, 2, "g")
+            transpose_wo(2 * r + 1, 1, "v")
+            next_tokens(r + 1, 1, "s")
+            products(d)
+            gate_tokens(r, 3, "v")
+            keep_clock(1 if DUMMY[r] else 0, DUMMY[r])
+            if r % 2 == 1:
+                swap_pair(r // 2)
+            load_round(r + 4)
+            for q, half, engine in PACKS[r]:
+                pack_pair(q, half, engine)
+                quantise_pair(q, half)
+                if half == 1:
+                    waiting.extend((m, n) for n in range((r + 1) // 2) for m in (2 * q, 2 * q + 1))
+            if r == 5:
+                waiting.extend((m, 2) for m in range(2))
+        quantise_wo(HALVES - 1)
+        waiting.extend((m, 3) for m in range(4))
+        waiting.extend((m, n) for m in (2, 3) for n in (2,))
+        waiting.extend((m, n) for m in (4, 5) for n in range(CHUNKS))
+        left = len(waiting)
+        products(left - 8)
         pack_pair(2, 0, "v")
-        run(2, 3)
-        gates(7, (0, 1))
         pack_pair(2, 1, "s")
         quantise_pair(2, 0)
-        run(3, 3)
-        gates(7, (2, 3))
-        swap_pair(3)
         quantise_pair(2, 1)
-        for n in range(CHUNKS):
-            run(4, n)
-        for n in range(CHUNKS):
-            run(5, n)
-            if n == 0:
-                pack_pair(3, 0, "s")
-                pack_pair(3, 1, "v")
-            if n == 1:
-                quantise_pair(3, 0)
-                quantise_pair(3, 1)
+        products(4)
+        pack_pair(3, 0, "v")
+        pack_pair(3, 1, "s")
+        quantise_pair(3, 0)
+        quantise_pair(3, 1)
+        products(4)
         for m in (6, 7):
             for n in range(CHUNKS):
                 run(m, n)
-        close(0)

@@ -29,9 +29,15 @@ HALF = 256
 HALVES = C // HALF
 QUAD = 32
 
-COUNTS = [(0,0,0,0)]*5 + [(1,1,1,1)]*3
-DUMMY = [512]*5+[0]*3
-PACKS = [(),(),(),((0,0,"v"),(0,1,"v")),(),((1,0,"v"),(1,1,"v")),(),()]
+COUNTS = [(0,0)]*5 + [(2,2),(2,2),(2,2)]
+WOE = "vvvvvsss"
+TE = "ssssssss"
+MUL = "vvvv"
+SORT = 8
+HEADD = 3
+BY_MATMUL = 6
+SE = ["ss"]*8
+EXTRA = {(4,0): ("K00v",), (4,1): ("K01v",), (4,2): ("Q00", "K02v",), (4,3): ("K03v", "Q01", "A02",), (5,0): ("K10v",), (5,1): ("K11s",), (5,2): ("K12v", "Q10",), (5,3): ("K13s",), (6,0): ("Q11", "A12", "C24",), (6,2): ("K20v",), (6,3): ("K21v",), (7,0): ("Q20", "K22v",), (7,1): ("K23s",), (7,2): ("Q21", "A23",), (8,0): ("P2", "C36", "P3", "K30v", "P1", "K31s", "K32v", "Q30", "P1", "K33s", "Q31", "A34",)}
 FLOPS = 2 * TOKENS * E * C + 2 * TOKENS * HEADS * P * P
 
 
@@ -43,19 +49,20 @@ def tile_gqaselfattention_pb_kernel(tc, attn, Wg, bg, Wo, bo, out):
     with ExitStack() as ctx:
         keep = ctx.enter_context(tc.tile_pool(name="keep", bufs=1))
         tok_pool = ctx.enter_context(tc.tile_pool(name="tok", bufs=5))
-        wo_pool = ctx.enter_context(tc.tile_pool(name="wo", bufs=10))
+        wo_pool = ctx.enter_context(tc.tile_pool(name="wo", bufs=7))
+        sorted_pool = ctx.enter_context(tc.tile_pool(name="sorted", bufs=4))
         feat_pool = ctx.enter_context(tc.tile_pool(name="feat", bufs=3))
-        gate_pool = ctx.enter_context(tc.tile_pool(name="gate", bufs=4))
+        gate_pool = ctx.enter_context(tc.tile_pool(name="gate", bufs=6))
         gated_pool = ctx.enter_context(tc.tile_pool(name="gated", bufs=2))
         swapped_pool = ctx.enter_context(tc.tile_pool(name="swapped", bufs=2))
-        packed_pool = ctx.enter_context(tc.tile_pool(name="packed", bufs=2))
+        packed_pool = ctx.enter_context(tc.tile_pool(name="packed", bufs=3))
         grouped_pool = ctx.enter_context(tc.tile_pool(name="grouped", bufs=3))
-        result_pool = ctx.enter_context(tc.tile_pool(name="result", bufs=7))
+        result_pool = ctx.enter_context(tc.tile_pool(name="result", bufs=4))
         block_banks = ctx.enter_context(tc.psum_pool(name="blocks", bufs=4))
         gate_banks = ctx.enter_context(tc.psum_pool(name="gates", bufs=2))
         product_banks = ctx.enter_context(tc.psum_pool(name="products", bufs=2))
 
-        ctx.enter_context(tc.manual_schedule(engines={mybir.EngineType.PE, mybir.EngineType.SP}))
+        ctx.enter_context(tc.manual_schedule())
         bo_all = keep.tile([P, C], BF16)
         wg_in = keep.tile([P, P], BF16)
         bg_col = keep.tile([P, 1], BF16)
@@ -98,6 +105,7 @@ def tile_gqaselfattention_pb_kernel(tc, attn, Wg, bg, Wo, bo, out):
         swapped_of = {}
         packed_of = {}
         grouped_of = {}
+        sorted_of = {}
 
         def transpose_tokens(m, i, engine):
             if i == 0:
@@ -106,11 +114,12 @@ def tile_gqaselfattention_pb_kernel(tc, attn, Wg, bg, Wo, bo, out):
                 bank = block_banks.tile([P, 8 * P], BF16, name="bank", tag="blocks")
                 for j in range(8):
                     head = 8 * i + j
-                    nc.tensor.transpose(
-                        out=bank[:, j * P : (j + 1) * P],
-                        in_=tokens_of[m][:, head * P : (head + 1) * P],
-                        identity=ident[:],
-                    )
+                    turned = bank[:, j * P : (j + 1) * P]
+                    block = tokens_of[m][:, head * P : (head + 1) * P]
+                    if m < BY_MATMUL:
+                        nc.tensor.matmul(out=turned, lhsT=block, rhs=ident[:], start=True, stop=True)
+                    else:
+                        nc.tensor.transpose(out=turned, in_=block, identity=ident[:])
                 copy = nc.vector.tensor_copy if engine == "v" else nc.scalar.copy
                 copy(out=feats_of[m][:, i * 8 * P : (i + 1) * 8 * P], in_=bank[:])
 
@@ -124,7 +133,7 @@ def tile_gqaselfattention_pb_kernel(tc, attn, Wg, bg, Wo, bo, out):
             nc.tensor.matmul(out=z[:], lhsT=wg_t[:], rhs=a_t, start=True, stop=True)
             gate = gate_pool.tile([P, 4 * P], F32, name="gate")
             nc.scalar.activation(out=gate[:], in_=z[:], func=SIGMOID, bias=bg_col[:, 0:1])
-            (nc.gpsimd if engine == "g" else nc.vector).tensor_tensor(
+            return lambda: (nc.gpsimd if engine == "g" else nc.vector).tensor_tensor(
                 out=h_t,
                 in0=gate[:].rearrange("p (h c) -> p h c", h=4),
                 in1=a_t.rearrange("p (h c) -> p h c", h=4),
@@ -143,12 +152,14 @@ def tile_gqaselfattention_pb_kernel(tc, attn, Wg, bg, Wo, bo, out):
                 if t < len(between):
                     between[t]()
 
-        def pack_pair(q, half, engine):
-            packed_of[q, half] = packed_pool.tile([P, 2 * PAIR * PACK], BF16, name="packed", align_bytes=64)
+        def pack_pair(q, g, engine):
+            if g % 2 == 0:
+                packed_of[q, g // 2] = packed_pool.tile([P, 2 * PAIR * PACK], BF16, name="packed", align_bytes=64)
+            cols = slice((g % 2) * PAIR * PACK, (g % 2 + 1) * PAIR * PACK)
             copy = nc.vector.tensor_copy if engine == "v" else nc.scalar.copy
             copy(
-                out=packed_of[q, half][:].rearrange("p (c t) -> p c t", t=PACK),
-                in_=swapped_of[q][:, :, 2 * half : 2 * half + 2, :].rearrange("p t g c -> p (g c) t"),
+                out=packed_of[q, g // 2][:, cols].rearrange("p (c t) -> p c t", t=PACK),
+                in_=swapped_of[q][:, :, g, :].rearrange("p t c -> p c t"),
             )
 
         def quantise_pair(q, half):
@@ -157,11 +168,21 @@ def tile_gqaselfattention_pb_kernel(tc, attn, Wg, bg, Wo, bo, out):
                 out=h_codes[:, q, cols].bitcast(FP8X4), scales=h_scales[:, q, cols], in_=packed_of[q, half][:]
             )
 
+        def sort_wo(s, engine="v"):
+            if s >= C // P:
+                return
+            sorted_of[s] = sorted_pool.tile([P, E], BF16, name="sorted")
+            copy = nc.vector.tensor_copy if engine == "v" else nc.scalar.copy
+            copy(
+                out=sorted_of[s][:].bitcast(F32).rearrange("r (g u p) -> r g u p", g=PASSES, u=2),
+                in_=wo_of[s][:].bitcast(F32).rearrange("r (g p u) -> r g u p", g=PASSES, u=2),
+            )
+
         def transpose_wo(s, b, engine):
             w = s // 2
             if s % 2 == 0 and b == 0:
                 grouped_of[w] = grouped_pool.tile([P, PASSES * HALF * PACK], BF16, name="grouped", align_bytes=64)
-            words_in = wo_of[s][:].bitcast(F32)
+            words_in = (sorted_of if s in sorted_of else wo_of)[s][:].bitcast(F32)
             words_out = grouped_of[w][:].bitcast(F32).rearrange("p (g r u) -> p g r u", g=PASSES, u=2)
             first = (s % 2) * P
             if True:
@@ -172,7 +193,9 @@ def tile_gqaselfattention_pb_kernel(tc, attn, Wg, bg, Wo, bo, out):
                         place = 2 * j + u
                         nc.tensor.transpose(
                             out=bank[:, place * P : (place + 1) * P],
-                            in_=words_in[:, 256 * g + u : 256 * (g + 1) : 2],
+                            in_=words_in[:, (2 * g + u) * P : (2 * g + u + 1) * P]
+                            if s in sorted_of
+                            else words_in[:, 256 * g + u : 256 * (g + 1) : 2],
                             identity=ident_words[:],
                         )
                 copy = nc.vector.tensor_copy if engine == "v" else nc.scalar.copy
@@ -232,11 +255,12 @@ def tile_gqaselfattention_pb_kernel(tc, attn, Wg, bg, Wo, bo, out):
 
         def keep_clock(count, width=CHUNK):
             for i in range(count):
-                nothing = gate_banks.tile([P, CHUNK], F32, name="z")
+                nothing = product_banks.tile([P, CHUNK], F32, name="acc")
                 nc.tensor.matmul(out=nothing[:, 0:width], lhsT=idle[:, 0:P], rhs=idle[:, 0:width], start=True, stop=True)
 
 
         waiting = []
+        later = []
 
         def products(count):
             for i in range(min(count, len(waiting))):
@@ -249,67 +273,76 @@ def tile_gqaselfattention_pb_kernel(tc, attn, Wg, bg, Wo, bo, out):
         def load_round(r):
             if r < TILES:
                 load_wo(2 * r)
-                if r + 1 < TILES:
-                    load_tokens(r + 1)
+                if r + 2 < TILES:
+                    load_tokens(r + 2)
                 load_wo(2 * r + 1)
 
+        def multiply():
+            while later:
+                later.pop(0)()
+
+        def extra(r, place):
+            for what in EXTRA.get((r, place), ()):
+                kind = what[0]
+                if kind == "K":
+                    pack_pair(int(what[1]), int(what[2]), what[3])
+                elif kind == "Q":
+                    quantise_pair(int(what[1]), int(what[2]))
+                elif kind == "A":
+                    q = int(what[1])
+                    waiting.extend((m, n) for n in range(int(what[2])) for m in (2 * q, 2 * q + 1))
+                elif kind == "C":
+                    waiting.extend((m, int(what[1])) for m in range(int(what[2])))
+                elif kind == "P":
+                    products(int(what[1:]))
+
         load_tokens(0)
-        for r in range(4):
+        load_tokens(1)
+        for r in range(3):
             load_round(r)
-            if r == 2:
+            if r == 1:
                 nc.sync.dma_start(out=bo_all[:], in_=bo.partition_broadcast(P))
-        keep_clock(5)
+        keep_clock(HEADD)
         set_up_gate()
         transpose_tokens(0, 0, "s")
-        keep_clock(1)
         transpose_tokens(0, 1, "v")
-        keep_clock(1)
+        later.append(gate_tokens(0, 0, "v"))
+        later.append(gate_tokens(0, 1, "g"))
+        transpose_tokens(1, 0, "v")
+        multiply()
+        later.append(gate_tokens(0, 2, "v"))
+        later.append(gate_tokens(0, 3, "g"))
+        transpose_tokens(1, 1, "v")
         for r in range(TILES):
-            a, b, c, d = COUNTS[r]
+            a, b = COUNTS[r]
+            tile = r + 1
             transpose_wo(2 * r, 0, "s")
-            products(a)
-            gate_tokens(r, 0, "g")
-            transpose_wo(2 * r, 1, "v")
-            next_tokens(r + 1, 0, "s")
-            products(b)
-            if r > 0:
-                quantise_wo(r - 1)
-            gate_tokens(r, 1, "v")
-            keep_clock(1 if DUMMY[r] else 0, DUMMY[r])
-            transpose_wo(2 * r + 1, 0, "s")
-            products(c)
-            gate_tokens(r, 2, "g")
-            transpose_wo(2 * r + 1, 1, "v")
-            next_tokens(r + 1, 1, "s")
-            products(d)
-            gate_tokens(r, 3, "v")
-            keep_clock(1 if DUMMY[r] else 0, DUMMY[r])
+            transpose_wo(2 * r, 1, WOE[r])
+            next_tokens(tile + 1, 0, "s")
+            multiply()
+            extra(r, 0)
             if r % 2 == 1:
                 swap_pair(r // 2)
-            load_round(r + 4)
-            for q, half, engine in PACKS[r]:
-                pack_pair(q, half, engine)
-                quantise_pair(q, half)
-                if half == 1:
-                    waiting.extend((m, n) for n in range((r + 1) // 2) for m in (2 * q, 2 * q + 1))
-            if r == 5:
-                waiting.extend((m, 2) for m in range(2))
+            load_round(r + 3)
+            for j in (0, 1) if tile < TILES else ():
+                later.append(gate_tokens(tile, j, MUL[j]))
+            products(a)
+            extra(r, 1)
+            if 2 * r + 2 >= SORT:
+                sort_wo(2 * r + 2, SE[r][0])
+            transpose_wo(2 * r + 1, 0, "s")
+            transpose_wo(2 * r + 1, 1, WOE[r])
+            next_tokens(tile + 1, 1, TE[r])
+            multiply()
+            if r > 0:
+                quantise_wo(r - 1)
+            extra(r, 2)
+            for j in (2, 3) if tile < TILES else ():
+                later.append(gate_tokens(tile, j, MUL[j]))
+            products(b)
+            extra(r, 3)
+            if 2 * r + 3 >= SORT:
+                sort_wo(2 * r + 3, SE[r][1])
         quantise_wo(HALVES - 1)
-        waiting.extend((m, 3) for m in range(4))
-        waiting.extend((m, n) for m in (2, 3) for n in (2,))
-        waiting.extend((m, n) for m in (4, 5) for n in range(CHUNKS))
-        left = len(waiting)
-        products(left - 8)
-        pack_pair(2, 0, "v")
-        pack_pair(2, 1, "s")
-        quantise_pair(2, 0)
-        quantise_pair(2, 1)
-        products(4)
-        pack_pair(3, 0, "v")
-        pack_pair(3, 1, "s")
-        quantise_pair(3, 0)
-        quantise_pair(3, 1)
-        products(4)
-        for m in (6, 7):
-            for n in range(CHUNKS):
-                run(m, n)
+        extra(8, 0)
+        products(len(waiting))

@@ -30,13 +30,11 @@ HALVES = C // HALF
 QUAD = 32
 
 COUNTS = [(0,0)]*5 + [(2,2),(2,2),(2,2)]
-WOE = "vvvvvsss"
+WOE = "vvvvssss"
 TE = "ssssssss"
 MUL = "vvvv"
-SORT = 8
 HEADD = 3
 BY_MATMUL = 6
-SE = ["ss"]*8
 EXTRA = {(4,0): ("K00v",), (4,1): ("K01v",), (4,2): ("Q00", "K02v",), (4,3): ("K03v", "Q01", "A02",), (5,0): ("K10v",), (5,1): ("K11s",), (5,2): ("K12v", "Q10",), (5,3): ("K13s",), (6,0): ("Q11", "A12", "C24",), (6,2): ("K20v",), (6,3): ("K21v",), (7,0): ("Q20", "K22v",), (7,1): ("K23s",), (7,2): ("Q21", "A23",), (8,0): ("P2", "C36", "P3", "K30v", "P1", "K31s", "K32v", "Q30", "P1", "K33s", "Q31", "A34",)}
 FLOPS = 2 * TOKENS * E * C + 2 * TOKENS * HEADS * P * P
 
@@ -49,15 +47,14 @@ def tile_gqaselfattention_pb_kernel(tc, attn, Wg, bg, Wo, bo, out):
     with ExitStack() as ctx:
         keep = ctx.enter_context(tc.tile_pool(name="keep", bufs=1))
         tok_pool = ctx.enter_context(tc.tile_pool(name="tok", bufs=5))
-        wo_pool = ctx.enter_context(tc.tile_pool(name="wo", bufs=7))
-        sorted_pool = ctx.enter_context(tc.tile_pool(name="sorted", bufs=4))
+        wo_pool = ctx.enter_context(tc.tile_pool(name="wo", bufs=10))
         feat_pool = ctx.enter_context(tc.tile_pool(name="feat", bufs=3))
         gate_pool = ctx.enter_context(tc.tile_pool(name="gate", bufs=6))
         gated_pool = ctx.enter_context(tc.tile_pool(name="gated", bufs=2))
         swapped_pool = ctx.enter_context(tc.tile_pool(name="swapped", bufs=2))
         packed_pool = ctx.enter_context(tc.tile_pool(name="packed", bufs=3))
         grouped_pool = ctx.enter_context(tc.tile_pool(name="grouped", bufs=3))
-        result_pool = ctx.enter_context(tc.tile_pool(name="result", bufs=4))
+        result_pool = ctx.enter_context(tc.tile_pool(name="result", bufs=6))
         block_banks = ctx.enter_context(tc.psum_pool(name="blocks", bufs=4))
         gate_banks = ctx.enter_context(tc.psum_pool(name="gates", bufs=2))
         product_banks = ctx.enter_context(tc.psum_pool(name="products", bufs=2))
@@ -105,7 +102,6 @@ def tile_gqaselfattention_pb_kernel(tc, attn, Wg, bg, Wo, bo, out):
         swapped_of = {}
         packed_of = {}
         grouped_of = {}
-        sorted_of = {}
 
         def transpose_tokens(m, i, engine):
             if i == 0:
@@ -168,21 +164,11 @@ def tile_gqaselfattention_pb_kernel(tc, attn, Wg, bg, Wo, bo, out):
                 out=h_codes[:, q, cols].bitcast(FP8X4), scales=h_scales[:, q, cols], in_=packed_of[q, half][:]
             )
 
-        def sort_wo(s, engine="v"):
-            if s >= C // P:
-                return
-            sorted_of[s] = sorted_pool.tile([P, E], BF16, name="sorted")
-            copy = nc.vector.tensor_copy if engine == "v" else nc.scalar.copy
-            copy(
-                out=sorted_of[s][:].bitcast(F32).rearrange("r (g u p) -> r g u p", g=PASSES, u=2),
-                in_=wo_of[s][:].bitcast(F32).rearrange("r (g p u) -> r g u p", g=PASSES, u=2),
-            )
-
         def transpose_wo(s, b, engine):
             w = s // 2
             if s % 2 == 0 and b == 0:
                 grouped_of[w] = grouped_pool.tile([P, PASSES * HALF * PACK], BF16, name="grouped", align_bytes=64)
-            words_in = (sorted_of if s in sorted_of else wo_of)[s][:].bitcast(F32)
+            words_in = wo_of[s][:].bitcast(F32)
             words_out = grouped_of[w][:].bitcast(F32).rearrange("p (g r u) -> p g r u", g=PASSES, u=2)
             first = (s % 2) * P
             if True:
@@ -193,9 +179,7 @@ def tile_gqaselfattention_pb_kernel(tc, attn, Wg, bg, Wo, bo, out):
                         place = 2 * j + u
                         nc.tensor.transpose(
                             out=bank[:, place * P : (place + 1) * P],
-                            in_=words_in[:, (2 * g + u) * P : (2 * g + u + 1) * P]
-                            if s in sorted_of
-                            else words_in[:, 256 * g + u : 256 * (g + 1) : 2],
+                            in_=words_in[:, 256 * g + u : 256 * (g + 1) : 2],
                             identity=ident_words[:],
                         )
                 copy = nc.vector.tensor_copy if engine == "v" else nc.scalar.copy
@@ -328,8 +312,6 @@ def tile_gqaselfattention_pb_kernel(tc, attn, Wg, bg, Wo, bo, out):
                 later.append(gate_tokens(tile, j, MUL[j]))
             products(a)
             extra(r, 1)
-            if 2 * r + 2 >= SORT:
-                sort_wo(2 * r + 2, SE[r][0])
             transpose_wo(2 * r + 1, 0, "s")
             transpose_wo(2 * r + 1, 1, WOE[r])
             next_tokens(tile + 1, 1, TE[r])
@@ -341,8 +323,6 @@ def tile_gqaselfattention_pb_kernel(tc, attn, Wg, bg, Wo, bo, out):
                 later.append(gate_tokens(tile, j, MUL[j]))
             products(b)
             extra(r, 3)
-            if 2 * r + 3 >= SORT:
-                sort_wo(2 * r + 3, SE[r][1])
         quantise_wo(HALVES - 1)
         extra(8, 0)
         products(len(waiting))

@@ -47,14 +47,14 @@ def tile_gqaselfattention_pb_kernel(tc, attn, Wg, bg, Wo, bo, out):
     with ExitStack() as ctx:
         keep = ctx.enter_context(tc.tile_pool(name="keep", bufs=1))
         tok_pool = ctx.enter_context(tc.tile_pool(name="tok", bufs=5))
-        wo_pool = ctx.enter_context(tc.tile_pool(name="wo", bufs=10))
+        wo_pool = ctx.enter_context(tc.tile_pool(name="wo", bufs=9))
         feat_pool = ctx.enter_context(tc.tile_pool(name="feat", bufs=3))
         gate_pool = ctx.enter_context(tc.tile_pool(name="gate", bufs=6))
         gated_pool = ctx.enter_context(tc.tile_pool(name="gated", bufs=2))
         swapped_pool = ctx.enter_context(tc.tile_pool(name="swapped", bufs=2))
         packed_pool = ctx.enter_context(tc.tile_pool(name="packed", bufs=3))
         grouped_pool = ctx.enter_context(tc.tile_pool(name="grouped", bufs=3))
-        result_pool = ctx.enter_context(tc.tile_pool(name="result", bufs=6))
+        result_pool = ctx.enter_context(tc.tile_pool(name="result", bufs=8))
         block_banks = ctx.enter_context(tc.psum_pool(name="blocks", bufs=4))
         gate_banks = ctx.enter_context(tc.psum_pool(name="gates", bufs=2))
         product_banks = ctx.enter_context(tc.psum_pool(name="products", bufs=2))
@@ -121,10 +121,10 @@ def tile_gqaselfattention_pb_kernel(tc, attn, Wg, bg, Wo, bo, out):
 
         def gate_tokens(m, j, engine):
             if m % 2 == 0 and j == 0:
-                gated_of[m // 2] = gated_pool.tile([P, HEADS, PAIR], BF16, name="gated")
+                gated_of[m // 2] = gated_pool.tile([P, 4, PASSES, PAIR], BF16, name="gated")
             a_t = feats_of[m][:, j * 4 * P : (j + 1) * 4 * P]
             first = (m % 2) * P
-            h_t = gated_of[m // 2][:, 4 * j : 4 * j + 4, first : first + P]
+            h_t = gated_of[m // 2][:, :, j, first : first + P]
             z = gate_banks.tile([P, 4 * P], F32, name="z")
             nc.tensor.matmul(out=z[:], lhsT=wg_t[:], rhs=a_t, start=True, stop=True)
             gate = gate_pool.tile([P, 4 * P], F32, name="gate")
@@ -138,12 +138,11 @@ def tile_gqaselfattention_pb_kernel(tc, attn, Wg, bg, Wo, bo, out):
 
         def swap_pair(q, between=()):
             swapped_of[q] = swapped_pool.tile([P, PACK, PASSES, PAIR], BF16, name="swapped")
-            heads = gated_of[q][:].rearrange("p (g i) c -> p i g c", i=4)
             for t in range(PACK):
                 for i in (0, 2, 1, 3):
                     nc.sync.dma_start(
-                        out=swapped_of[q][QUAD * i : QUAD * (i + 1), t, :, :],
-                        in_=heads[t : P : PACK, i, :, :],
+                        out=swapped_of[q][QUAD * i : QUAD * (i + 1), t, :, :].rearrange("p g c -> p (g c)"),
+                        in_=gated_of[q][t : P : PACK, i, :, :].rearrange("p g c -> p (g c)"),
                     )
                 if t < len(between):
                     between[t]()

@@ -29,6 +29,7 @@ HALF = 256
 HALVES = C // HALF
 QUAD = 32
 
+ZALT = 5
 COUNTS = [(0,0)]*5 + [(2,2),(2,2),(2,2)]
 WOE = "vvvvssss"
 TE = "ssssssss"
@@ -68,7 +69,10 @@ def tile_gqaselfattention_pb_kernel(tc, attn, Wg, bg, Wo, bo, out):
 
         def load_tokens(m):
             tokens_of[m] = tok_pool.tile([P, E], BF16, name="tokens")
-            nc.sync.dma_start(out=tokens_of[m][:], in_=attn_rows[m * P : (m + 1) * P, :])
+            width = E // 2 if m == 0 else E
+            for first in range(0, E, width):
+                cols = slice(first, first + width)
+                nc.sync.dma_start(out=tokens_of[m][:, cols], in_=attn_rows[m * P : (m + 1) * P, cols])
 
         def load_wo(s):
             wo_of[s] = wo_pool.tile([P, E], BF16, name="wo_rows")
@@ -125,7 +129,10 @@ def tile_gqaselfattention_pb_kernel(tc, attn, Wg, bg, Wo, bo, out):
             a_t = feats_of[m][:, j * 4 * P : (j + 1) * 4 * P]
             first = (m % 2) * P
             h_t = gated_of[m // 2][:, :, j, first : first + P]
-            z = gate_banks.tile([P, 4 * P], F32, name="z")
+            if m < ZALT and j >= 2:
+                z = product_banks.tile([P, CHUNK], F32, name="acc")
+            else:
+                z = gate_banks.tile([P, 4 * P], F32, name="z")
             nc.tensor.matmul(out=z[:], lhsT=wg_t[:], rhs=a_t, start=True, stop=True)
             gate = gate_pool.tile([P, 4 * P], F32, name="gate")
             nc.scalar.activation(out=gate[:], in_=z[:], func=SIGMOID, bias=bg_col[:, 0:1])
@@ -196,9 +203,12 @@ def tile_gqaselfattention_pb_kernel(tc, attn, Wg, bg, Wo, bo, out):
                     in_=grouped_of[w][:, g * HALF * PACK : (g + 1) * HALF * PACK],
                 )
 
-        def product(m, n):
+        def product(m, n, spare=False):
             cols = slice(n * CHUNK, (n + 1) * CHUNK)
-            acc = product_banks.tile([P, CHUNK], F32, name="acc")
+            if spare:
+                acc = gate_banks.tile([P, CHUNK], F32, name="z")
+            else:
+                acc = product_banks.tile([P, CHUNK], F32, name="acc")
             for g in range(PASSES):
                 first = g * PAIR + (m % 2) * P
                 toks = slice(first, first + P)
@@ -225,8 +235,8 @@ def tile_gqaselfattention_pb_kernel(tc, attn, Wg, bg, Wo, bo, out):
             while len(open_products) > left:
                 finish_product(*open_products.pop(0))
 
-        def run(m, n):
-            open_products.append(product(m, n))
+        def run(m, n, spare=False):
+            open_products.append(product(m, n, spare))
             close(0)
 
         def gates(m, js):
@@ -245,9 +255,9 @@ def tile_gqaselfattention_pb_kernel(tc, attn, Wg, bg, Wo, bo, out):
         waiting = []
         later = []
 
-        def products(count):
+        def products(count, banks=1):
             for i in range(min(count, len(waiting))):
-                run(*waiting.pop(0))
+                run(*waiting.pop(0), spare=(i % banks == 1))
 
         def next_tokens(m, i, engine):
             if m < TILES:
@@ -277,7 +287,7 @@ def tile_gqaselfattention_pb_kernel(tc, attn, Wg, bg, Wo, bo, out):
                 elif kind == "C":
                     waiting.extend((m, int(what[1])) for m in range(int(what[2])))
                 elif kind == "P":
-                    products(int(what[1:]))
+                    products(int(what[1:]), 2)
 
         load_tokens(0)
         load_tokens(1)
@@ -309,7 +319,7 @@ def tile_gqaselfattention_pb_kernel(tc, attn, Wg, bg, Wo, bo, out):
             load_round(r + 3)
             for j in (0, 1) if tile < TILES else ():
                 later.append(gate_tokens(tile, j, MUL[j]))
-            products(a)
+            products(a, 2 if r >= 7 else 1)
             extra(r, 1)
             transpose_wo(2 * r + 1, 0, "s")
             transpose_wo(2 * r + 1, 1, WOE[r])
@@ -320,8 +330,8 @@ def tile_gqaselfattention_pb_kernel(tc, attn, Wg, bg, Wo, bo, out):
             extra(r, 2)
             for j in (2, 3) if tile < TILES else ():
                 later.append(gate_tokens(tile, j, MUL[j]))
-            products(b)
+            products(b, 2 if r >= 6 else 1)
             extra(r, 3)
         quantise_wo(HALVES - 1)
         extra(8, 0)
-        products(len(waiting))
+        products(len(waiting), 2)

@@ -32,7 +32,7 @@ QUAD = 32
 ZALT = 5
 COUNTS = [(0,0)]*5 + [(2,2),(2,2),(2,2)]
 WOE = "vvvvssss"
-TE = "ssssssss"
+TE = "vsvsssss"
 MUL = "vvvv"
 HEADD = 3
 BY_MATMUL = 6
@@ -96,10 +96,10 @@ def tile_gqaselfattention_pb_kernel(tc, attn, Wg, bg, Wo, bo, out):
             nc.tensor.transpose(out=setup[:, 0:P], in_=wg_in[:], identity=ident[:])
             nc.vector.tensor_copy(out=wg_t[:], in_=setup[:, 0:P])
 
-        h_codes = keep.tile([P, PAIRS, PASSES * PAIR], U32, align_bytes=64)
-        h_scales = keep.tile([P, PAIRS, PASSES * PAIR], U8, align_bytes=64)
-        wo_codes = keep.tile([P, PASSES, C], U32, align_bytes=64)
-        wo_scales = keep.tile([P, PASSES, C], U8, align_bytes=64)
+        h_codes = keep.tile([P, PAIRS, PASSES * PAIR], U32, align_bytes=256)
+        h_scales = keep.tile([P, PAIRS, PASSES * PAIR], U8, align_bytes=256)
+        wo_codes = keep.tile([P, PASSES, C], U32, align_bytes=256)
+        wo_scales = keep.tile([P, PASSES, C], U8, align_bytes=256)
 
         feats_of = {}
         gated_of = {}

@@ -32,11 +32,11 @@ QUAD = 32
 ZALT = 5
 COUNTS = [(0,0)]*5 + [(2,2),(2,2),(2,2)]
 WOE = "vvvvssss"
-TE = "vsvsssss"
+TE = "vvvsssss"
 MUL = "vvvv"
 HEADD = 3
 BY_MATMUL = 6
-EXTRA = {(4,0): ("K00v",), (4,1): ("K01v",), (4,2): ("Q00", "K02v",), (4,3): ("K03v", "Q01", "A02",), (5,0): ("K10v",), (5,1): ("K11s",), (5,2): ("K12v", "Q10",), (5,3): ("K13s",), (6,0): ("Q11", "A12", "C24",), (6,2): ("K20v",), (6,3): ("K21v",), (7,0): ("Q20", "K22v",), (7,1): ("K23s",), (7,2): ("Q21", "A23",), (8,0): ("P2", "C36", "P3", "K30v", "P1", "K31s", "K32v", "Q30", "P1", "K33s", "Q31", "A34",)}
+EXTRA = {(4,0): ("K00v",), (4,1): ("K01v",), (4,2): ("Q00", "K02v",), (4,3): ("K03v", "Q01", "A02",), (5,0): ("K10v", "K11s",), (5,1): ("K12v",), (5,2): ("Q10", "K13s",), (5,3): ("Q11", "A12", "C24",), (6,2): ("K20v",), (6,3): ("K21v",), (7,0): ("Q20", "K22v",), (7,1): ("K23s",), (7,2): ("Q21", "A23",), (8,0): ("P2", "C36", "P3", "K30v", "P1", "K31s", "K32v", "Q30", "P1", "K33s", "Q31", "A34",)}
 FLOPS = 2 * TOKENS * E * C + 2 * TOKENS * HEADS * P * P
 
 
@@ -203,8 +203,8 @@ def tile_gqaselfattention_pb_kernel(tc, attn, Wg, bg, Wo, bo, out):
                     in_=grouped_of[w][:, g * HALF * PACK : (g + 1) * HALF * PACK],
                 )
 
-        def product(m, n, spare=False):
-            cols = slice(n * CHUNK, (n + 1) * CHUNK)
+        def product(m, n, spare=False, first_col=0, width=CHUNK):
+            cols = slice(n * CHUNK + first_col, n * CHUNK + first_col + width)
             if spare:
                 acc = gate_banks.tile([P, CHUNK], F32, name="z")
             else:
@@ -213,7 +213,7 @@ def tile_gqaselfattention_pb_kernel(tc, attn, Wg, bg, Wo, bo, out):
                 first = g * PAIR + (m % 2) * P
                 toks = slice(first, first + P)
                 nc.tensor.matmul_mx(
-                    out=acc[:],
+                    out=acc[:, 0:width],
                     lhsT=h_codes[:, m // 2, toks].bitcast(FP8X4),
                     lhsT_scale=h_scales[:, m // 2, toks],
                     rhs=wo_codes[:, g, cols].bitcast(FP8X4),
@@ -221,13 +221,13 @@ def tile_gqaselfattention_pb_kernel(tc, attn, Wg, bg, Wo, bo, out):
                     start=(g == 0),
                     stop=(g == PASSES - 1),
                 )
-            return m, n, acc
+            return m, cols, acc[:, 0:width]
 
-        def finish_product(m, n, acc):
-            cols = slice(n * CHUNK, (n + 1) * CHUNK)
+        def finish_product(m, cols, acc):
+            width = cols.stop - cols.start
             result = result_pool.tile([P, CHUNK], F32, name="result")
-            nc.vector.tensor_tensor(out=result[:], in0=acc[:], in1=bo_all[:, cols], op=ADD)
-            nc.sync.dma_start(out=out_rows[m * P : (m + 1) * P, cols], in_=result[:])
+            nc.vector.tensor_tensor(out=result[:, 0:width], in0=acc, in1=bo_all[:, cols], op=ADD)
+            nc.sync.dma_start(out=out_rows[m * P : (m + 1) * P, cols], in_=result[:, 0:width])
 
         open_products = []
 
@@ -235,8 +235,8 @@ def tile_gqaselfattention_pb_kernel(tc, attn, Wg, bg, Wo, bo, out):
             while len(open_products) > left:
                 finish_product(*open_products.pop(0))
 
-        def run(m, n, spare=False):
-            open_products.append(product(m, n, spare))
+        def run(m, n, spare=False, first_col=0, width=CHUNK):
+            open_products.append(product(m, n, spare, first_col, width))
             close(0)
 
         def gates(m, js):
@@ -334,4 +334,7 @@ def tile_gqaselfattention_pb_kernel(tc, attn, Wg, bg, Wo, bo, out):
             extra(r, 3)
         quantise_wo(HALVES - 1)
         extra(8, 0)
-        products(len(waiting), 2)
+        products(len(waiting) - 1, 2)
+        last = waiting.pop(0)
+        run(*last, spare=True, first_col=0, width=CHUNK // 2)
+        run(*last, spare=False, first_col=CHUNK // 2, width=CHUNK // 2)

from contextlib import ExitStack

import concourse.mybir as mybir
from concourse.masks import make_identity

BF16 = mybir.dt.bfloat16
F32 = mybir.dt.float32
U32 = mybir.dt.uint32
U8 = mybir.dt.uint8
FP8X4 = mybir.dt.float8_e4m3fn_x4
SIGMOID = mybir.ActivationFunctionType.Sigmoid
MULT = mybir.AluOpType.mult
ADD = mybir.AluOpType.add

P = 128
TOKENS = 4 * 256
HEADS = 16
E = HEADS * P
C = 2048
PACK = 4
K_PASS = P * PACK
PASSES = E // K_PASS
TILES = TOKENS // P
PAIR = 2 * P
PAIRS = TOKENS // PAIR
CHUNK = 512
CHUNKS = C // CHUNK
HALF = 256
HALVES = C // HALF
QUAD = 32

ZALT = 5
COUNTS = [(0,0)]*5 + [(2,2),(2,2),(2,2)]
WOE = "vvvvssss"
TE = "vvvsssss"
MUL = "vvvv"
HEADD = 3
BY_MATMUL = 6
EXTRA = {(4,0): ("K00v",), (4,1): ("K01v",), (4,2): ("Q00", "K02v",), (4,3): ("K03v", "Q01", "A02",), (5,0): ("K10v", "K11s",), (5,1): ("K12v",), (5,2): ("Q10", "K13s",), (5,3): ("Q11", "A12", "C24",), (6,2): ("K20v",), (6,3): ("K21v",), (7,0): ("Q20", "K22v",), (7,1): ("K23s",), (7,2): ("Q21", "A23",), (8,0): ("P2", "C36", "P3", "K30v", "P1", "K31s", "K32v", "Q30", "P1", "K33s", "Q31", "A34",)}
FLOPS = 2 * TOKENS * E * C + 2 * TOKENS * HEADS * P * P


def tile_gqaselfattention_pb_kernel(tc, attn, Wg, bg, Wo, bo, out):
    nc = tc.nc
    attn_rows = attn.rearrange("b t h d -> (b t) (h d)")
    out_rows = out.rearrange("b t c -> (b t) c")

    with ExitStack() as ctx:
        keep = ctx.enter_context(tc.tile_pool(name="keep", bufs=1))
        tok_pool = ctx.enter_context(tc.tile_pool(name="tok", bufs=5))
        wo_pool = ctx.enter_context(tc.tile_pool(name="wo", bufs=9))
        feat_pool = ctx.enter_context(tc.tile_pool(name="feat", bufs=3))
        gate_pool = ctx.enter_context(tc.tile_pool(name="gate", bufs=6))
        gated_pool = ctx.enter_context(tc.tile_pool(name="gated", bufs=2))
        swapped_pool = ctx.enter_context(tc.tile_pool(name="swapped", bufs=2))
        packed_pool = ctx.enter_context(tc.tile_pool(name="packed", bufs=3))
        grouped_pool = ctx.enter_context(tc.tile_pool(name="grouped", bufs=3))
        result_pool = ctx.enter_context(tc.tile_pool(name="result", bufs=8))
        block_banks = ctx.enter_context(tc.psum_pool(name="blocks", bufs=4))
        gate_banks = ctx.enter_context(tc.psum_pool(name="gates", bufs=2))
        product_banks = ctx.enter_context(tc.psum_pool(name="products", bufs=2))

        ctx.enter_context(tc.manual_schedule())
        bo_all = keep.tile([P, C], BF16)
        wg_in = keep.tile([P, P], BF16)
        bg_col = keep.tile([P, 1], BF16)
        tokens_of = {}
        wo_of = {}

        def load_tokens(m):
            tokens_of[m] = tok_pool.tile([P, E], BF16, name="tokens")
            width = E // 2 if m == 0 else E
            for first in range(0, E, width):
                cols = slice(first, first + width)
                nc.sync.dma_start(out=tokens_of[m][:, cols], in_=attn_rows[m * P : (m + 1) * P, cols])

        def load_wo(s):
            wo_of[s] = wo_pool.tile([P, E], BF16, name="wo_rows")
            nc.sync.dma_start(out=wo_of[s][:], in_=Wo[s * P : (s + 1) * P, :])

        ident = keep.tile([P, P], BF16)
        make_identity(nc, ident[:])
        ident_words = keep.tile([P, P], F32)
        make_identity(nc, ident_words[:])
        nc.scalar.dma_start(out=wg_in[:], in_=Wg)
        nc.scalar.dma_start(out=bg_col[:], in_=bg.rearrange("(f o) -> f o", o=1))

        warm = keep.tile([P, 1], F32)
        nc.vector.memset(warm[:], 0.0)
        nc.scalar.activation(out=warm[:], in_=warm[:], func=SIGMOID)

        wg_t = keep.tile([P, P], BF16)

        def set_up_gate():
            setup = block_banks.tile([P, 8 * P], BF16, name="setup", tag="blocks")
            nc.tensor.transpose(out=setup[:, 0:P], in_=wg_in[:], identity=ident[:])
            nc.vector.tensor_copy(out=wg_t[:], in_=setup[:, 0:P])

        h_codes = keep.tile([P, PAIRS, PASSES * PAIR], U32, align_bytes=256)
        h_scales = keep.tile([P, PAIRS, PASSES * PAIR], U8, align_bytes=256)
        wo_codes = keep.tile([P, PASSES, C], U32, align_bytes=256)
        wo_scales = keep.tile([P, PASSES, C], U8, align_bytes=256)

        feats_of = {}
        gated_of = {}
        swapped_of = {}
        packed_of = {}
        grouped_of = {}

        def transpose_tokens(m, i, engine):
            if i == 0:
                feats_of[m] = feat_pool.tile([P, HEADS * P], BF16, name="feats")
            if True:
                bank = block_banks.tile([P, 8 * P], BF16, name="bank", tag="blocks")
                for j in range(8):
                    head = 8 * i + j
                    turned = bank[:, j * P : (j + 1) * P]
                    block = tokens_of[m][:, head * P : (head + 1) * P]
                    if m < BY_MATMUL:
                        nc.tensor.matmul(out=turned, lhsT=block, rhs=ident[:], start=True, stop=True)
                    else:
                        nc.tensor.transpose(out=turned, in_=block, identity=ident[:])
                copy = nc.vector.tensor_copy if engine == "v" else nc.scalar.copy
                copy(out=feats_of[m][:, i * 8 * P : (i + 1) * 8 * P], in_=bank[:])

        def gate_tokens(m, j, engine):
            if m % 2 == 0 and j == 0:
                gated_of[m // 2] = gated_pool.tile([P, 4, PASSES, PAIR], BF16, name="gated")
            a_t = feats_of[m][:, j * 4 * P : (j + 1) * 4 * P]
            first = (m % 2) * P
            h_t = gated_of[m // 2][:, :, j, first : first + P]
            if m < ZALT and j >= 2:
                z = product_banks.tile([P, CHUNK], F32, name="acc")
            else:
                z = gate_banks.tile([P, 4 * P], F32, name="z")
            nc.tensor.matmul(out=z[:], lhsT=wg_t[:], rhs=a_t, start=True, stop=True)
            gate = gate_pool.tile([P, 4 * P], F32, name="gate")
            nc.scalar.activation(out=gate[:], in_=z[:], func=SIGMOID, bias=bg_col[:, 0:1])
            return lambda: (nc.gpsimd if engine == "g" else nc.vector).tensor_tensor(
                out=h_t,
                in0=gate[:].rearrange("p (h c) -> p h c", h=4),
                in1=a_t.rearrange("p (h c) -> p h c", h=4),
                op=MULT,
            )

        def swap_pair(q, between=()):
            swapped_of[q] = swapped_pool.tile([P, PACK, PASSES, PAIR], BF16, name="swapped")
            for t in range(PACK):
                for i in (0, 2, 1, 3):
                    nc.sync.dma_start(
                        out=swapped_of[q][QUAD * i : QUAD * (i + 1), t, :, :].rearrange("p g c -> p (g c)"),
                        in_=gated_of[q][t : P : PACK, i, :, :].rearrange("p g c -> p (g c)"),
                    )
                if t < len(between):
                    between[t]()

        def pack_pair(q, g, engine):
            if g % 2 == 0:
                packed_of[q, g // 2] = packed_pool.tile([P, 2 * PAIR * PACK], BF16, name="packed", align_bytes=64)
            cols = slice((g % 2) * PAIR * PACK, (g % 2 + 1) * PAIR * PACK)
            copy = nc.vector.tensor_copy if engine == "v" else nc.scalar.copy
            copy(
                out=packed_of[q, g // 2][:, cols].rearrange("p (c t) -> p c t", t=PACK),
                in_=swapped_of[q][:, :, g, :].rearrange("p t c -> p c t"),
            )

        def quantise_pair(q, half):
            cols = slice(half * 2 * PAIR, (half + 1) * 2 * PAIR)
            nc.vector.quantize_mx(
                out=h_codes[:, q, cols].bitcast(FP8X4), scales=h_scales[:, q, cols], in_=packed_of[q, half][:]
            )

        def transpose_wo(s, b, engine):
            w = s // 2
            if s % 2 == 0 and b == 0:
                grouped_of[w] = grouped_pool.tile([P, PASSES * HALF * PACK], BF16, name="grouped", align_bytes=64)
            words_in = wo_of[s][:].bitcast(F32)
            words_out = grouped_of[w][:].bitcast(F32).rearrange("p (g r u) -> p g r u", g=PASSES, u=2)
            first = (s % 2) * P
            if True:
                bank = block_banks.tile([P, 4 * P], F32, name="bank", tag="blocks")
                for j in range(2):
                    g = 2 * b + j
                    for u in range(2):
                        place = 2 * j + u
                        nc.tensor.transpose(
                            out=bank[:, place * P : (place + 1) * P],
                            in_=words_in[:, 256 * g + u : 256 * (g + 1) : 2],
                            identity=ident_words[:],
                        )
                copy = nc.vector.tensor_copy if engine == "v" else nc.scalar.copy
                copy(
                    out=words_out[:, 2 * b : 2 * b + 2, first : first + P, :],
                    in_=bank[:].rearrange("p (g u r) -> p g r u", g=2, u=2),
                )

        def quantise_wo(w):
            cols = slice(w * HALF, (w + 1) * HALF)
            for g in range(PASSES):
                nc.vector.quantize_mx(
                    out=wo_codes[:, g, cols].bitcast(FP8X4),
                    scales=wo_scales[:, g, cols],
                    in_=grouped_of[w][:, g * HALF * PACK : (g + 1) * HALF * PACK],
                )

        def product(m, n, spare=False, first_col=0, width=CHUNK):
            cols = slice(n * CHUNK + first_col, n * CHUNK + first_col + width)
            if spare:
                acc = gate_banks.tile([P, CHUNK], F32, name="z")
            else:
                acc = product_banks.tile([P, CHUNK], F32, name="acc")
            for g in range(PASSES):
                first = g * PAIR + (m % 2) * P
                toks = slice(first, first + P)
                nc.tensor.matmul_mx(
                    out=acc[:, 0:width],
                    lhsT=h_codes[:, m // 2, toks].bitcast(FP8X4),
                    lhsT_scale=h_scales[:, m // 2, toks],
                    rhs=wo_codes[:, g, cols].bitcast(FP8X4),
                    rhs_scale=wo_scales[:, g, cols],
                    start=(g == 0),
                    stop=(g == PASSES - 1),
                )
            return m, cols, acc[:, 0:width]

        def finish_product(m, cols, acc):
            width = cols.stop - cols.start
            result = result_pool.tile([P, CHUNK], F32, name="result")
            nc.vector.tensor_tensor(out=result[:, 0:width], in0=acc, in1=bo_all[:, cols], op=ADD)
            nc.sync.dma_start(out=out_rows[m * P : (m + 1) * P, cols], in_=result[:, 0:width])

        open_products = []

        def close(left):
            while len(open_products) > left:
                finish_product(*open_products.pop(0))

        def run(m, n, spare=False, first_col=0, width=CHUNK):
            open_products.append(product(m, n, spare, first_col, width))
            close(0)

        def gates(m, js):
            for j in js:
                gate_tokens(m, j)

        idle = keep.tile([P, CHUNK], BF16)
        nc.vector.memset(idle[:], 0.0)

        def keep_clock(count, width=CHUNK):
            for i in range(count):
                nothing = product_banks.tile([P, CHUNK], F32, name="acc")
                nc.tensor.matmul(out=nothing[:, 0:width], lhsT=idle[:, 0:P], rhs=idle[:, 0:width], start=True, stop=True)


        waiting = []
        later = []

        def products(count, banks=1):
            for i in range(min(count, len(waiting))):
                run(*waiting.pop(0), spare=(i % banks == 1))

        def next_tokens(m, i, engine):
            if m < TILES:
                transpose_tokens(m, i, engine)

        def load_round(r):
            if r < TILES:
                load_wo(2 * r)
                if r + 2 < TILES:
                    load_tokens(r + 2)
                load_wo(2 * r + 1)

        def multiply():
            while later:
                later.pop(0)()

        def extra(r, place):
            for what in EXTRA.get((r, place), ()):
                kind = what[0]
                if kind == "K":
                    pack_pair(int(what[1]), int(what[2]), what[3])
                elif kind == "Q":
                    quantise_pair(int(what[1]), int(what[2]))
                elif kind == "A":
                    q = int(what[1])
                    waiting.extend((m, n) for n in range(int(what[2])) for m in (2 * q, 2 * q + 1))
                elif kind == "C":
                    waiting.extend((m, int(what[1])) for m in range(int(what[2])))
                elif kind == "P":
                    products(int(what[1:]), 2)

        load_tokens(0)
        load_tokens(1)
        for r in range(3):
            load_round(r)
            if r == 1:
                nc.sync.dma_start(out=bo_all[:], in_=bo.partition_broadcast(P))
        keep_clock(HEADD)
        set_up_gate()
        transpose_tokens(0, 0, "s")
        transpose_tokens(0, 1, "v")
        later.append(gate_tokens(0, 0, "v"))
        later.append(gate_tokens(0, 1, "g"))
        transpose_tokens(1, 0, "v")
        multiply()
        later.append(gate_tokens(0, 2, "v"))
        later.append(gate_tokens(0, 3, "g"))
        transpose_tokens(1, 1, "v")
        for r in range(TILES):
            a, b = COUNTS[r]
            tile = r + 1
            transpose_wo(2 * r, 0, "s")
            transpose_wo(2 * r, 1, WOE[r])
            next_tokens(tile + 1, 0, "s")
            multiply()
            extra(r, 0)
            if r % 2 == 1:
                swap_pair(r // 2)
            load_round(r + 3)
            for j in (0, 1) if tile < TILES else ():
                later.append(gate_tokens(tile, j, MUL[j]))
            products(a, 2 if r >= 7 else 1)
            extra(r, 1)
            transpose_wo(2 * r + 1, 0, "s")
            transpose_wo(2 * r + 1, 1, WOE[r])
            next_tokens(tile + 1, 1, TE[r])
            multiply()
            if r > 0:
                quantise_wo(r - 1)
            extra(r, 2)
            for j in (2, 3) if tile < TILES else ():
                later.append(gate_tokens(tile, j, MUL[j]))
            products(b, 2 if r >= 6 else 1)
            extra(r, 3)
        quantise_wo(HALVES - 1)
        extra(8, 0)
        products(len(waiting) - 1, 2)
        last = waiting.pop(0)
        run(*last, spare=True, first_col=0, width=CHUNK // 2)
        run(*last, spare=False, first_col=CHUNK // 2, width=CHUNK // 2)
